import numpy as np
import ml_dtypes


def mxq(x, axis, fmt="e4m3"):
    dtype, down = {"e4m3": (ml_dtypes.float8_e4m3fn, 7), "e5m2": (ml_dtypes.float8_e5m2, 14)}[fmt]
    v = np.moveaxis(np.asarray(x, np.float32).astype(ml_dtypes.bfloat16).astype(np.float64), axis, -1)
    blocks = v.reshape(v.shape[:-1] + (-1, 32))
    amax = np.abs(blocks).max(-1, keepdims=True)
    byte = np.maximum(np.where(amax > 0, np.frexp(amax)[1] - 1 + 127, 0) - down, 1)
    scale = np.exp2(byte - 127.0)
    codes = (blocks / scale).astype(np.float32).astype(dtype).astype(np.float64)
    return np.moveaxis((codes * scale).reshape(v.shape), -1, axis)


WIDE = False


def mx_kscale(k):
    if not WIDE:
        return np.ones(k)
    levels = np.array([10, -10, 5, -5, 0])
    a = np.random.permutation(np.resize(levels, k // 512 * 4)).reshape(k // 512, 4)
    idx = np.arange(k)
    return np.exp2(a[idx // 512, idx % 128 // 32])


BF16 = ml_dtypes.bfloat16


def bf(x):
    return np.asarray(x, np.float32).astype(BF16)


def f64(x):
    return np.asarray(x).astype(np.float64)


N, F, D1, D2, D3, D4, D5 = 512, 64, 16, 1024, 512, 512, 128
EDGE_PROB = 0.003
LEAKY_SLOPE = 0.01
DEG = 2.0 * EDGE_PROB * N


def sigmoid(v):
    return 1.0 / (1.0 + np.exp(-v))


def adjacency():
    u = np.random.uniform(size=(N, N))
    a = np.where(u < EDGE_PROB, 1.0, 0.0)
    return np.maximum(a, a.T)


def setup_inputs():
    s = mx_kscale(N)
    g = np.random.standard_normal((N, D4)) * 0.75
    h = np.maximum(g, LEAKY_SLOPE * g)
    return {"h4": bf(h / s[:, None]),
            "A": bf(adjacency() * s),
            "W4": bf(np.random.standard_normal((D4, D5)) * 0.8 / np.sqrt(D4 * DEG))}


def reference(h4, A, W4):
    t5 = mxq(f64(A), 1, "e4m3") @ mxq(f64(h4), 0, "e4m3")
    a5 = mxq(t5, 1, "e4m3") @ mxq(f64(W4), 0, "e4m3")
    z = sigmoid(a5)
    return t5, a5, z

@@ -1,0 +1,168 @@
+from contextlib import ExitStack
+
+import concourse.mybir as mybir
+from concourse.masks import make_identity
+
+BF16 = mybir.dt.bfloat16
+F32 = mybir.dt.float32
+U32 = mybir.dt.uint32
+U8 = mybir.dt.uint8
+FP8X4 = mybir.dt.float8_e4m3fn_x4
+SIGMOID = mybir.ActivationFunctionType.Sigmoid
+
+P = 128
+PACK = 4
+NODES = 512
+FEATURES = 512
+OUT_FEATURES = 128
+GROUPS = NODES // P
+HALF = GROUPS // 2
+
+FLOPS = 2 * NODES * NODES * FEATURES + 2 * NODES * FEATURES * OUT_FEATURES
+
+
+def block(i, width=P):
+    return slice(i * width, (i + 1) * width)
+
+
+def tile_gcn_kron_pb_s_kernel(tc, h4, A, W4, t5_out, a5_out, z_out):
+    nc = tc.nc
+    with ExitStack() as ctx:
+        keep = ctx.enter_context(tc.tile_pool(name="keep", bufs=1))
+        psum = ctx.enter_context(tc.psum_pool(name="psum", bufs=8))
+
+        h4_rows = keep.tile([P, PACK, FEATURES], BF16)
+        nc.sync.dma_start(
+            out=h4_rows[:].rearrange("p (u e) c -> p u e c", e=2),
+            in_=h4.rearrange("(u p e) c -> p u e c", p=P, e=2),
+        )
+        a_rows = keep.tile([P, GROUPS, NODES], BF16)
+        a_view = A.rearrange("(r j) k -> r j k", j=GROUPS)
+        for b in range(2):
+            nc.sync.dma_start(out=a_rows[:, block(b, HALF), :], in_=a_view[:, block(b, HALF), :])
+        w4_rows = keep.tile([P, PACK, OUT_FEATURES], BF16)
+        nc.scalar.dma_start(out=w4_rows[:], in_=W4.rearrange("(t p) d -> p t d", p=P))
+
+        ident = keep.tile([P, P], F32)
+        make_identity(nc, ident[:])
+        table_warmer = keep.tile([P, 1], F32)
+        nc.vector.memset(table_warmer[:], 0.0)
+        nc.scalar.activation(out=table_warmer[:], in_=table_warmer[:], func=SIGMOID)
+
+        h4_grouped = keep.tile([P, FEATURES, PACK], BF16, align_bytes=64)
+        h4_codes = keep.tile([P, FEATURES], U32, align_bytes=64)
+        h4_scales = keep.tile([P, FEATURES], U8, align_bytes=64)
+        half_cols = FEATURES // 2
+        for b, copy in enumerate((nc.vector.tensor_copy, nc.scalar.copy)):
+            cols = block(b, half_cols)
+            copy(
+                out=h4_grouped[:, cols, :].rearrange("p (c i) t -> p c t i", i=4),
+                in_=h4_rows[:, :, cols].rearrange("p t (c i) -> p c t i", i=4),
+            )
+        for b in range(2):
+            cols = block(b, half_cols)
+            nc.vector.quantize_mx(
+                out=h4_codes[:, cols].bitcast(FP8X4),
+                scales=h4_scales[:, cols],
+                in_=h4_grouped[:, cols, :].rearrange("p c t -> p (c t)"),
+            )
+
+        w4_grouped = keep.tile([P, OUT_FEATURES, PACK], BF16, align_bytes=64)
+        w4_codes = keep.tile([P, OUT_FEATURES], U32, align_bytes=64)
+        w4_scales = keep.tile([P, OUT_FEATURES], U8, align_bytes=64)
+        nc.vector.tensor_copy(
+            out=w4_grouped[:].rearrange("p (d i) t -> p d t i", i=4),
+            in_=w4_rows[:].rearrange("p t (d i) -> p d t i", i=4),
+        )
+        nc.vector.quantize_mx(
+            out=w4_codes[:].bitcast(FP8X4),
+            scales=w4_scales[:],
+            in_=w4_grouped[:].rearrange("p d t -> p (d t)"),
+        )
+
+        a_words = a_rows[:].rearrange("r j k -> r (j k)").bitcast(F32)
+        words_per_row = NODES // 2
+        at_grouped = keep.tile([P, GROUPS * P * PACK], BF16, align_bytes=64)
+        at_grouped_words = at_grouped[:].bitcast(F32).rearrange(
+            "p (j r u) -> p j r u", j=GROUPS, u=2
+        )
+        at_codes = keep.tile([P, NODES], U32, align_bytes=64)
+        at_scales = keep.tile([P, NODES], U8, align_bytes=64)
+        for b, copy in enumerate((nc.scalar.copy, nc.vector.tensor_copy)):
+            at_bank = psum.tile([P, HALF, 2, P], F32, tag="bank")
+            for jj in range(HALF):
+                for u in range(2):
+                    first = (b * HALF + jj) * words_per_row + u * P
+                    nc.tensor.transpose(at_bank[:, jj, u, :], a_words[:, first : first + P], ident[:])
+            copy(
+                out=at_grouped_words[:, block(b, HALF), :, :],
+                in_=at_bank[:].rearrange("p j u r -> p j r u"),
+            )
+            nc.vector.quantize_mx(
+                out=at_codes[:, block(b, HALF * P)].bitcast(FP8X4),
+                scales=at_scales[:, block(b, HALF * P)],
+                in_=at_grouped[:, block(b, HALF * P * PACK)],
+            )
+
+        t5t_grouped = keep.tile([P, GROUPS, P, PACK], BF16, align_bytes=64)
+        t5t_codes = keep.tile([P, NODES], U32, align_bytes=64)
+        t5t_scales = keep.tile([P, NODES], U8, align_bytes=64)
+        for j in range(GROUPS):
+            t5t_bank = psum.tile([P, PACK, P], F32, tag="bank")
+            for t in range(PACK):
+                nc.tensor.matmul_mx(
+                    out=t5t_bank[:, t, :],
+                    lhsT=h4_codes[:, block(t)].bitcast(FP8X4),
+                    lhsT_scale=h4_scales[:, block(t)],
+                    rhs=at_codes[:, block(j)].bitcast(FP8X4),
+                    rhs_scale=at_scales[:, block(j)],
+                    start=True,
+                    stop=True,
+                )
+            copy = nc.vector.tensor_copy if j % 2 == 0 else nc.scalar.copy
+            copy(out=t5t_grouped[:, j, :, :], in_=t5t_bank[:].rearrange("p t r -> p r t"))
+        for b in range(2):
+            nc.vector.quantize_mx(
+                out=t5t_codes[:, block(b, HALF * P)].bitcast(FP8X4),
+                scales=t5t_scales[:, block(b, HALF * P)],
+                in_=t5t_grouped[:, block(b, HALF), :, :].rearrange("p j r t -> p (j r t)"),
+            )
+
+        t5_sb = keep.tile([P, GROUPS, FEATURES], F32)
+        t5_view = t5_out.rearrange("(r j) f -> r j f", j=GROUPS)
+        for j in range(GROUPS):
+            t5_bank = psum.tile([P, FEATURES], F32, tag="bank")
+            nc.tensor.matmul_mx(
+                out=t5_bank[:],
+                lhsT=at_codes[:, block(j)].bitcast(FP8X4),
+                lhsT_scale=at_scales[:, block(j)],
+                rhs=h4_codes[:].bitcast(FP8X4),
+                rhs_scale=h4_scales[:],
+                start=True,
+                stop=True,
+            )
+            copy = nc.scalar.copy if j % 2 == 0 else nc.vector.tensor_copy
+            copy(out=t5_sb[:, j, :], in_=t5_bank[:])
+            nc.sync.dma_start(out=t5_view[:, j, :], in_=t5_sb[:, j, :])
+
+        a5_sb = keep.tile([P, GROUPS, OUT_FEATURES], F32)
+        z_sb = keep.tile([P, GROUPS, OUT_FEATURES], F32)
+        for b in range(2):
+            a5_bank = psum.tile([P, HALF, OUT_FEATURES], F32, tag="bank")
+            for jj in range(HALF):
+                j = b * HALF + jj
+                nc.tensor.matmul_mx(
+                    out=a5_bank[:, jj, :],
+                    lhsT=t5t_codes[:, block(j)].bitcast(FP8X4),
+                    lhsT_scale=t5t_scales[:, block(j)],
+                    rhs=w4_codes[:].bitcast(FP8X4),
+                    rhs_scale=w4_scales[:],
+                    start=True,
+                    stop=True,
+                )
+            nc.vector.tensor_copy(out=a5_sb[:, block(b, HALF), :], in_=a5_bank[:])
+            nc.scalar.activation(
+                out=z_sb[:, block(b, HALF), :], in_=a5_sb[:, block(b, HALF), :], func=SIGMOID
+            )
+        nc.sync.dma_start(out=a5_out.rearrange("(r j) d -> r j d", j=GROUPS), in_=a5_sb[:])
+        nc.sync.dma_start(out=z_out.rearrange("(r j) d -> r j d", j=GROUPS), in_=z_sb[:])

@@ -16,7 +16,7 @@ NODES = 512
 FEATURES = 512
 OUT_FEATURES = 128
 GROUPS = NODES // P
-HALF = GROUPS // 2
+PAIR = 2
 
 FLOPS = 2 * NODES * NODES * FEATURES + 2 * NODES * FEATURES * OUT_FEATURES
 
@@ -29,7 +29,9 @@ def tile_gcn_kron_pb_s_kernel(tc, h4, A, W4, t5_out, a5_out, z_out):
     nc = tc.nc
     with ExitStack() as ctx:
         keep = ctx.enter_context(tc.tile_pool(name="keep", bufs=1))
-        psum = ctx.enter_context(tc.psum_pool(name="psum", bufs=8))
+        psum = ctx.enter_context(tc.psum_pool(name="psum", bufs=6))
+        psum_a5 = ctx.enter_context(tc.psum_pool(name="psum_a5", bufs=2))
+        ctx.enter_context(tc.manual_schedule())
 
         h4_rows = keep.tile([P, PACK, FEATURES], BF16)
         nc.sync.dma_start(
@@ -38,10 +40,10 @@ def tile_gcn_kron_pb_s_kernel(tc, h4, A, W4, t5_out, a5_out, z_out):
         )
         a_rows = keep.tile([P, GROUPS, NODES], BF16)
         a_view = A.rearrange("(r j) k -> r j k", j=GROUPS)
-        for b in range(2):
-            nc.sync.dma_start(out=a_rows[:, block(b, HALF), :], in_=a_view[:, block(b, HALF), :])
+        for j in range(GROUPS):
+            nc.sync.dma_start(out=a_rows[:, j, :], in_=a_view[:, j, :])
         w4_rows = keep.tile([P, PACK, OUT_FEATURES], BF16)
-        nc.scalar.dma_start(out=w4_rows[:], in_=W4.rearrange("(t p) d -> p t d", p=P))
+        nc.sync.dma_start(out=w4_rows[:], in_=W4.rearrange("(t p) d -> p t d", p=P))
 
         ident = keep.tile([P, P], F32)
         make_identity(nc, ident[:])
@@ -52,19 +54,44 @@ def tile_gcn_kron_pb_s_kernel(tc, h4, A, W4, t5_out, a5_out, z_out):
         h4_grouped = keep.tile([P, FEATURES, PACK], BF16, align_bytes=64)
         h4_codes = keep.tile([P, FEATURES], U32, align_bytes=64)
         h4_scales = keep.tile([P, FEATURES], U8, align_bytes=64)
-        half_cols = FEATURES // 2
-        for b, copy in enumerate((nc.vector.tensor_copy, nc.scalar.copy)):
-            cols = block(b, half_cols)
+        quarter = FEATURES // 4
+        for copy, cols in (
+            (nc.vector.tensor_copy, slice(0, 2 * quarter)),
+            (nc.vector.tensor_copy, slice(2 * quarter, 3 * quarter)),
+            (nc.scalar.copy, slice(3 * quarter, FEATURES)),
+        ):
             copy(
                 out=h4_grouped[:, cols, :].rearrange("p (c i) t -> p c t i", i=4),
                 in_=h4_rows[:, :, cols].rearrange("p t (c i) -> p c t i", i=4),
             )
-        for b in range(2):
-            cols = block(b, half_cols)
+        for cols in (slice(0, 2 * quarter), slice(2 * quarter, FEATURES)):
             nc.vector.quantize_mx(
                 out=h4_codes[:, cols].bitcast(FP8X4),
                 scales=h4_scales[:, cols],
                 in_=h4_grouped[:, cols, :].rearrange("p c t -> p (c t)"),
+            )
+
+        a_words = a_rows[:].rearrange("r j k -> r (j k)").bitcast(F32)
+        words_per_row = NODES // 2
+        at_grouped = keep.tile([P, GROUPS * P * PACK], BF16, align_bytes=64)
+        at_grouped_words = at_grouped[:].bitcast(F32).rearrange(
+            "p (j r u) -> p j r u", j=GROUPS, u=2
+        )
+        at_codes = keep.tile([P, NODES], U32, align_bytes=64)
+        at_scales = keep.tile([P, NODES], U8, align_bytes=64)
+        for j in range(GROUPS):
+            at_bank = psum.tile([P, 2, P], F32, tag="bank")
+            for u in range(2):
+                first = j * words_per_row + u * P
+                nc.tensor.transpose(at_bank[:, u, :], a_words[:, first : first + P], ident[:])
+            nc.scalar.copy(
+                out=at_grouped_words[:, j, :, :], in_=at_bank[:].rearrange("p u r -> p r u")
+            )
+        for j in range(GROUPS):
+            nc.vector.quantize_mx(
+                out=at_codes[:, block(j)].bitcast(FP8X4),
+                scales=at_scales[:, block(j)],
+                in_=at_grouped[:, block(j, P * PACK)],
             )
 
         w4_grouped = keep.tile([P, OUT_FEATURES, PACK], BF16, align_bytes=64)
@@ -80,56 +107,19 @@ def tile_gcn_kron_pb_s_kernel(tc, h4, A, W4, t5_out, a5_out, z_out):
             in_=w4_grouped[:].rearrange("p d t -> p (d t)"),
         )
 
-        a_words = a_rows[:].rearrange("r j k -> r (j k)").bitcast(F32)
-        words_per_row = NODES // 2
-        at_grouped = keep.tile([P, GROUPS * P * PACK], BF16, align_bytes=64)
-        at_grouped_words = at_grouped[:].bitcast(F32).rearrange(
-            "p (j r u) -> p j r u", j=GROUPS, u=2
-        )
-        at_codes = keep.tile([P, NODES], U32, align_bytes=64)
-        at_scales = keep.tile([P, NODES], U8, align_bytes=64)
-        for b, copy in enumerate((nc.scalar.copy, nc.vector.tensor_copy)):
-            at_bank = psum.tile([P, HALF, 2, P], F32, tag="bank")
-            for jj in range(HALF):
-                for u in range(2):
-                    first = (b * HALF + jj) * words_per_row + u * P
-                    nc.tensor.transpose(at_bank[:, jj, u, :], a_words[:, first : first + P], ident[:])
-            copy(
-                out=at_grouped_words[:, block(b, HALF), :, :],
-                in_=at_bank[:].rearrange("p j u r -> p j r u"),
-            )
-            nc.vector.quantize_mx(
-                out=at_codes[:, block(b, HALF * P)].bitcast(FP8X4),
-                scales=at_scales[:, block(b, HALF * P)],
-                in_=at_grouped[:, block(b, HALF * P * PACK)],
-            )
-
+        t5_sb = keep.tile([P, GROUPS, FEATURES], F32)
+        t5_view = t5_out.rearrange("(r j) f -> r j f", j=GROUPS)
         t5t_grouped = keep.tile([P, GROUPS, P, PACK], BF16, align_bytes=64)
         t5t_codes = keep.tile([P, NODES], U32, align_bytes=64)
         t5t_scales = keep.tile([P, NODES], U8, align_bytes=64)
-        for j in range(GROUPS):
-            t5t_bank = psum.tile([P, PACK, P], F32, tag="bank")
-            for t in range(PACK):
-                nc.tensor.matmul_mx(
-                    out=t5t_bank[:, t, :],
-                    lhsT=h4_codes[:, block(t)].bitcast(FP8X4),
-                    lhsT_scale=h4_scales[:, block(t)],
-                    rhs=at_codes[:, block(j)].bitcast(FP8X4),
-                    rhs_scale=at_scales[:, block(j)],
-                    start=True,
-                    stop=True,
-                )
-            copy = nc.vector.tensor_copy if j % 2 == 0 else nc.scalar.copy
-            copy(out=t5t_grouped[:, j, :, :], in_=t5t_bank[:].rearrange("p t r -> p r t"))
-        for b in range(2):
+
+        def quantise_t5t(j):
             nc.vector.quantize_mx(
-                out=t5t_codes[:, block(b, HALF * P)].bitcast(FP8X4),
-                scales=t5t_scales[:, block(b, HALF * P)],
-                in_=t5t_grouped[:, block(b, HALF), :, :].rearrange("p j r t -> p (j r t)"),
+                out=t5t_codes[:, block(j)].bitcast(FP8X4),
+                scales=t5t_scales[:, block(j)],
+                in_=t5t_grouped[:, j, :, :].rearrange("p r t -> p (r t)"),
             )
 
-        t5_sb = keep.tile([P, GROUPS, FEATURES], F32)
-        t5_view = t5_out.rearrange("(r j) f -> r j f", j=GROUPS)
         for j in range(GROUPS):
             t5_bank = psum.tile([P, FEATURES], F32, tag="bank")
             nc.tensor.matmul_mx(
@@ -141,16 +131,34 @@ def tile_gcn_kron_pb_s_kernel(tc, h4, A, W4, t5_out, a5_out, z_out):
                 start=True,
                 stop=True,
             )
-            copy = nc.scalar.copy if j % 2 == 0 else nc.vector.tensor_copy
-            copy(out=t5_sb[:, j, :], in_=t5_bank[:])
+            nc.scalar.copy(out=t5_sb[:, j, :], in_=t5_bank[:])
             nc.sync.dma_start(out=t5_view[:, j, :], in_=t5_sb[:, j, :])
+            t5t_bank = psum.tile([P, PACK, P], F32, tag="bank")
+            for t in range(PACK):
+                nc.tensor.matmul_mx(
+                    out=t5t_bank[:, t, :],
+                    lhsT=h4_codes[:, block(t)].bitcast(FP8X4),
+                    lhsT_scale=h4_scales[:, block(t)],
+                    rhs=at_codes[:, block(j)].bitcast(FP8X4),
+                    rhs_scale=at_scales[:, block(j)],
+                    start=True,
+                    stop=True,
+                )
+            nc.vector.tensor_copy(
+                out=t5t_grouped[:, j, :, :], in_=t5t_bank[:].rearrange("p t r -> p r t")
+            )
+            if j > 0:
+                quantise_t5t(j - 1)
+        quantise_t5t(GROUPS - 1)
 
         a5_sb = keep.tile([P, GROUPS, OUT_FEATURES], F32)
         z_sb = keep.tile([P, GROUPS, OUT_FEATURES], F32)
-        for b in range(2):
-            a5_bank = psum.tile([P, HALF, OUT_FEATURES], F32, tag="bank")
-            for jj in range(HALF):
-                j = b * HALF + jj
+        a5_view = a5_out.rearrange("(r j) d -> r j d", j=GROUPS)
+        z_view = z_out.rearrange("(r j) d -> r j d", j=GROUPS)
+        for b in range(GROUPS // PAIR):
+            a5_bank = psum_a5.tile([P, PAIR, OUT_FEATURES], F32)
+            for jj in range(PAIR):
+                j = b * PAIR + jj
                 nc.tensor.matmul_mx(
                     out=a5_bank[:, jj, :],
                     lhsT=t5t_codes[:, block(j)].bitcast(FP8X4),
@@ -160,9 +168,8 @@ def tile_gcn_kron_pb_s_kernel(tc, h4, A, W4, t5_out, a5_out, z_out):
                     start=True,
                     stop=True,
                 )
-            nc.vector.tensor_copy(out=a5_sb[:, block(b, HALF), :], in_=a5_bank[:])
-            nc.scalar.activation(
-                out=z_sb[:, block(b, HALF), :], in_=a5_sb[:, block(b, HALF), :], func=SIGMOID
-            )
-        nc.sync.dma_start(out=a5_out.rearrange("(r j) d -> r j d", j=GROUPS), in_=a5_sb[:])
-        nc.sync.dma_start(out=z_out.rearrange("(r j) d -> r j d", j=GROUPS), in_=z_sb[:])
+            groups = block(b, PAIR)
+            nc.scalar.activation(out=z_sb[:, groups, :], in_=a5_bank[:], func=SIGMOID)
+            nc.sync.dma_start(out=z_view[:, groups, :], in_=z_sb[:, groups, :])
+            nc.scalar.copy(out=a5_sb[:, groups, :], in_=a5_bank[:])
+            nc.sync.dma_start(out=a5_view[:, groups, :], in_=a5_sb[:, groups, :])

@@ -17,6 +17,8 @@ FEATURES = 512
 OUT_FEATURES = 128
 GROUPS = NODES // P
 PAIR = 2
+IDLE_WHILE_LOADING = 20
+IDLE_AFTER_TRANSPOSES = 4
 
 FLOPS = 2 * NODES * NODES * FEATURES + 2 * NODES * FEATURES * OUT_FEATURES
 
@@ -50,6 +52,29 @@ def tile_gcn_kron_pb_s_kernel(tc, h4, A, W4, t5_out, a5_out, z_out):
         table_warmer = keep.tile([P, 1], F32)
         nc.vector.memset(table_warmer[:], 0.0)
         nc.scalar.activation(out=table_warmer[:], in_=table_warmer[:], func=SIGMOID)
+
+        idle_values = keep.tile([P, P * PACK], BF16, align_bytes=64)
+        idle_codes = keep.tile([P, P], U32, align_bytes=64)
+        idle_scales = keep.tile([P, P], U8, align_bytes=64)
+        nc.vector.memset(idle_values[:], 0.0)
+        nc.vector.quantize_mx(
+            out=idle_codes[:].bitcast(FP8X4), scales=idle_scales[:], in_=idle_values[:]
+        )
+        idle_bank = psum.tile([P, PACK, P], F32, tag="bank")
+
+        def idle_passes(count):
+            for i in range(count):
+                nc.tensor.matmul_mx(
+                    out=idle_bank[:, i % PACK, :],
+                    lhsT=idle_codes[:].bitcast(FP8X4),
+                    lhsT_scale=idle_scales[:],
+                    rhs=idle_codes[:].bitcast(FP8X4),
+                    rhs_scale=idle_scales[:],
+                    start=True,
+                    stop=True,
+                )
+
+        idle_passes(IDLE_WHILE_LOADING)
 
         h4_grouped = keep.tile([P, FEATURES, PACK], BF16, align_bytes=64)
         h4_codes = keep.tile([P, FEATURES], U32, align_bytes=64)
@@ -87,6 +112,7 @@ def tile_gcn_kron_pb_s_kernel(tc, h4, A, W4, t5_out, a5_out, z_out):
             nc.scalar.copy(
                 out=at_grouped_words[:, j, :, :], in_=at_bank[:].rearrange("p u r -> p r u")
             )
+        idle_passes(IDLE_AFTER_TRANSPOSES)
         for j in range(GROUPS):
             nc.vector.quantize_mx(
                 out=at_codes[:, block(j)].bitcast(FP8X4),

@@ -17,8 +17,7 @@ FEATURES = 512
 OUT_FEATURES = 128
 GROUPS = NODES // P
 PAIR = 2
-IDLE_WHILE_LOADING = 20
-IDLE_AFTER_TRANSPOSES = 4
+IDLE_PASSES = 16
 
 FLOPS = 2 * NODES * NODES * FEATURES + 2 * NODES * FEATURES * OUT_FEATURES
 
@@ -31,8 +30,7 @@ def tile_gcn_kron_pb_s_kernel(tc, h4, A, W4, t5_out, a5_out, z_out):
     nc = tc.nc
     with ExitStack() as ctx:
         keep = ctx.enter_context(tc.tile_pool(name="keep", bufs=1))
-        psum = ctx.enter_context(tc.psum_pool(name="psum", bufs=6))
-        psum_a5 = ctx.enter_context(tc.psum_pool(name="psum_a5", bufs=2))
+        psum = ctx.enter_context(tc.psum_pool(name="psum", bufs=8))
         ctx.enter_context(tc.manual_schedule())
 
         h4_rows = keep.tile([P, PACK, FEATURES], BF16)
@@ -61,35 +59,31 @@ def tile_gcn_kron_pb_s_kernel(tc, h4, A, W4, t5_out, a5_out, z_out):
             out=idle_codes[:].bitcast(FP8X4), scales=idle_scales[:], in_=idle_values[:]
         )
         idle_bank = psum.tile([P, PACK, P], F32, tag="bank")
-
-        def idle_passes(count):
-            for i in range(count):
-                nc.tensor.matmul_mx(
-                    out=idle_bank[:, i % PACK, :],
-                    lhsT=idle_codes[:].bitcast(FP8X4),
-                    lhsT_scale=idle_scales[:],
-                    rhs=idle_codes[:].bitcast(FP8X4),
-                    rhs_scale=idle_scales[:],
-                    start=True,
-                    stop=True,
-                )
-
-        idle_passes(IDLE_WHILE_LOADING)
+        for i in range(IDLE_PASSES):
+            nc.tensor.matmul_mx(
+                out=idle_bank[:, i % PACK, :],
+                lhsT=idle_codes[:].bitcast(FP8X4),
+                lhsT_scale=idle_scales[:],
+                rhs=idle_codes[:].bitcast(FP8X4),
+                rhs_scale=idle_scales[:],
+                start=True,
+                stop=True,
+            )
 
         h4_grouped = keep.tile([P, FEATURES, PACK], BF16, align_bytes=64)
         h4_codes = keep.tile([P, FEATURES], U32, align_bytes=64)
         h4_scales = keep.tile([P, FEATURES], U8, align_bytes=64)
-        quarter = FEATURES // 4
+        eighth = FEATURES // 8
         for copy, cols in (
-            (nc.vector.tensor_copy, slice(0, 2 * quarter)),
-            (nc.vector.tensor_copy, slice(2 * quarter, 3 * quarter)),
-            (nc.scalar.copy, slice(3 * quarter, FEATURES)),
+            (nc.vector.tensor_copy, slice(0, 4 * eighth)),
+            (nc.vector.tensor_copy, slice(4 * eighth, 5 * eighth)),
+            (nc.scalar.copy, slice(5 * eighth, FEATURES)),
         ):
             copy(
                 out=h4_grouped[:, cols, :].rearrange("p (c i) t -> p c t i", i=4),
                 in_=h4_rows[:, :, cols].rearrange("p t (c i) -> p c t i", i=4),
             )
-        for cols in (slice(0, 2 * quarter), slice(2 * quarter, FEATURES)):
+        for cols in (slice(0, 4 * eighth), slice(4 * eighth, FEATURES)):
             nc.vector.quantize_mx(
                 out=h4_codes[:, cols].bitcast(FP8X4),
                 scales=h4_scales[:, cols],
@@ -112,7 +106,6 @@ def tile_gcn_kron_pb_s_kernel(tc, h4, A, W4, t5_out, a5_out, z_out):
             nc.scalar.copy(
                 out=at_grouped_words[:, j, :, :], in_=at_bank[:].rearrange("p u r -> p r u")
             )
-        idle_passes(IDLE_AFTER_TRANSPOSES)
         for j in range(GROUPS):
             nc.vector.quantize_mx(
                 out=at_codes[:, block(j)].bitcast(FP8X4),
@@ -123,14 +116,9 @@ def tile_gcn_kron_pb_s_kernel(tc, h4, A, W4, t5_out, a5_out, z_out):
         w4_grouped = keep.tile([P, OUT_FEATURES, PACK], BF16, align_bytes=64)
         w4_codes = keep.tile([P, OUT_FEATURES], U32, align_bytes=64)
         w4_scales = keep.tile([P, OUT_FEATURES], U8, align_bytes=64)
-        nc.vector.tensor_copy(
+        nc.scalar.copy(
             out=w4_grouped[:].rearrange("p (d i) t -> p d t i", i=4),
             in_=w4_rows[:].rearrange("p t (d i) -> p d t i", i=4),
-        )
-        nc.vector.quantize_mx(
-            out=w4_codes[:].bitcast(FP8X4),
-            scales=w4_scales[:],
-            in_=w4_grouped[:].rearrange("p d t -> p (d t)"),
         )
 
         t5_sb = keep.tile([P, GROUPS, FEATURES], F32)
@@ -147,18 +135,6 @@ def tile_gcn_kron_pb_s_kernel(tc, h4, A, W4, t5_out, a5_out, z_out):
             )
 
         for j in range(GROUPS):
-            t5_bank = psum.tile([P, FEATURES], F32, tag="bank")
-            nc.tensor.matmul_mx(
-                out=t5_bank[:],
-                lhsT=at_codes[:, block(j)].bitcast(FP8X4),
-                lhsT_scale=at_scales[:, block(j)],
-                rhs=h4_codes[:].bitcast(FP8X4),
-                rhs_scale=h4_scales[:],
-                start=True,
-                stop=True,
-            )
-            nc.scalar.copy(out=t5_sb[:, j, :], in_=t5_bank[:])
-            nc.sync.dma_start(out=t5_view[:, j, :], in_=t5_sb[:, j, :])
             t5t_bank = psum.tile([P, PACK, P], F32, tag="bank")
             for t in range(PACK):
                 nc.tensor.matmul_mx(
@@ -173,8 +149,26 @@ def tile_gcn_kron_pb_s_kernel(tc, h4, A, W4, t5_out, a5_out, z_out):
             nc.vector.tensor_copy(
                 out=t5t_grouped[:, j, :, :], in_=t5t_bank[:].rearrange("p t r -> p r t")
             )
+            t5_bank = psum.tile([P, FEATURES], F32, tag="bank")
+            nc.tensor.matmul_mx(
+                out=t5_bank[:],
+                lhsT=at_codes[:, block(j)].bitcast(FP8X4),
+                lhsT_scale=at_scales[:, block(j)],
+                rhs=h4_codes[:].bitcast(FP8X4),
+                rhs_scale=h4_scales[:],
+                start=True,
+                stop=True,
+            )
+            nc.scalar.copy(out=t5_sb[:, j, :], in_=t5_bank[:])
+            nc.sync.dma_start(out=t5_view[:, j, :], in_=t5_sb[:, j, :])
             if j > 0:
                 quantise_t5t(j - 1)
+            else:
+                nc.vector.quantize_mx(
+                    out=w4_codes[:].bitcast(FP8X4),
+                    scales=w4_scales[:],
+                    in_=w4_grouped[:].rearrange("p d t -> p (d t)"),
+                )
         quantise_t5t(GROUPS - 1)
 
         a5_sb = keep.tile([P, GROUPS, OUT_FEATURES], F32)
@@ -182,20 +176,22 @@ def tile_gcn_kron_pb_s_kernel(tc, h4, A, W4, t5_out, a5_out, z_out):
         a5_view = a5_out.rearrange("(r j) d -> r j d", j=GROUPS)
         z_view = z_out.rearrange("(r j) d -> r j d", j=GROUPS)
         for b in range(GROUPS // PAIR):
-            a5_bank = psum_a5.tile([P, PAIR, OUT_FEATURES], F32)
+            a5_for_z = psum.tile([P, PAIR, OUT_FEATURES], F32, tag="bank")
+            a5_for_store = psum.tile([P, PAIR, OUT_FEATURES], F32, tag="bank")
             for jj in range(PAIR):
                 j = b * PAIR + jj
-                nc.tensor.matmul_mx(
-                    out=a5_bank[:, jj, :],
-                    lhsT=t5t_codes[:, block(j)].bitcast(FP8X4),
-                    lhsT_scale=t5t_scales[:, block(j)],
-                    rhs=w4_codes[:].bitcast(FP8X4),
-                    rhs_scale=w4_scales[:],
-                    start=True,
-                    stop=True,
-                )
+                for a5_bank in (a5_for_z, a5_for_store):
+                    nc.tensor.matmul_mx(
+                        out=a5_bank[:, jj, :],
+                        lhsT=t5t_codes[:, block(j)].bitcast(FP8X4),
+                        lhsT_scale=t5t_scales[:, block(j)],
+                        rhs=w4_codes[:].bitcast(FP8X4),
+                        rhs_scale=w4_scales[:],
+                        start=True,
+                        stop=True,
+                    )
             groups = block(b, PAIR)
-            nc.scalar.activation(out=z_sb[:, groups, :], in_=a5_bank[:], func=SIGMOID)
+            nc.scalar.activation(out=z_sb[:, groups, :], in_=a5_for_z[:], func=SIGMOID)
             nc.sync.dma_start(out=z_view[:, groups, :], in_=z_sb[:, groups, :])
-            nc.scalar.copy(out=a5_sb[:, groups, :], in_=a5_bank[:])
+            nc.vector.tensor_copy(out=a5_sb[:, groups, :], in_=a5_for_store[:])
             nc.sync.dma_start(out=a5_view[:, groups, :], in_=a5_sb[:, groups, :])

@@ -17,7 +17,8 @@ FEATURES = 512
 OUT_FEATURES = 128
 GROUPS = NODES // P
 PAIR = 2
-IDLE_PASSES = 16
+IDLE_WHILE_LOADING = 12
+IDLE_AFTER_TRANSPOSES = 4
 
 FLOPS = 2 * NODES * NODES * FEATURES + 2 * NODES * FEATURES * OUT_FEATURES
 
@@ -59,16 +60,20 @@ def tile_gcn_kron_pb_s_kernel(tc, h4, A, W4, t5_out, a5_out, z_out):
             out=idle_codes[:].bitcast(FP8X4), scales=idle_scales[:], in_=idle_values[:]
         )
         idle_bank = psum.tile([P, PACK, P], F32, tag="bank")
-        for i in range(IDLE_PASSES):
-            nc.tensor.matmul_mx(
-                out=idle_bank[:, i % PACK, :],
-                lhsT=idle_codes[:].bitcast(FP8X4),
-                lhsT_scale=idle_scales[:],
-                rhs=idle_codes[:].bitcast(FP8X4),
-                rhs_scale=idle_scales[:],
-                start=True,
-                stop=True,
-            )
+
+        def idle_passes(count):
+            for i in range(count):
+                nc.tensor.matmul_mx(
+                    out=idle_bank[:, i % PACK, :],
+                    lhsT=idle_codes[:].bitcast(FP8X4),
+                    lhsT_scale=idle_scales[:],
+                    rhs=idle_codes[:].bitcast(FP8X4),
+                    rhs_scale=idle_scales[:],
+                    start=True,
+                    stop=True,
+                )
+
+        idle_passes(IDLE_WHILE_LOADING)
 
         h4_grouped = keep.tile([P, FEATURES, PACK], BF16, align_bytes=64)
         h4_codes = keep.tile([P, FEATURES], U32, align_bytes=64)
@@ -106,6 +111,7 @@ def tile_gcn_kron_pb_s_kernel(tc, h4, A, W4, t5_out, a5_out, z_out):
             nc.scalar.copy(
                 out=at_grouped_words[:, j, :, :], in_=at_bank[:].rearrange("p u r -> p r u")
             )
+        idle_passes(IDLE_AFTER_TRANSPOSES)
         for j in range(GROUPS):
             nc.vector.quantize_mx(
                 out=at_codes[:, block(j)].bitcast(FP8X4),

@@ -17,7 +17,7 @@ FEATURES = 512
 OUT_FEATURES = 128
 GROUPS = NODES // P
 PAIR = 2
-IDLE_WHILE_LOADING = 12
+IDLE_WHILE_LOADING = 18
 IDLE_AFTER_TRANSPOSES = 4
 
 FLOPS = 2 * NODES * NODES * FEATURES + 2 * NODES * FEATURES * OUT_FEATURES
@@ -46,18 +46,18 @@ def tile_gcn_kron_pb_s_kernel(tc, h4, A, W4, t5_out, a5_out, z_out):
         w4_rows = keep.tile([P, PACK, OUT_FEATURES], BF16)
         nc.sync.dma_start(out=w4_rows[:], in_=W4.rearrange("(t p) d -> p t d", p=P))
 
+        table_warmer = keep.tile([P, 1], F32)
+        nc.gpsimd.memset(table_warmer[:], 0.0)
+        nc.scalar.activation(out=table_warmer[:], in_=table_warmer[:], func=SIGMOID)
         ident = keep.tile([P, P], F32)
         make_identity(nc, ident[:])
-        table_warmer = keep.tile([P, 1], F32)
-        nc.vector.memset(table_warmer[:], 0.0)
-        nc.scalar.activation(out=table_warmer[:], in_=table_warmer[:], func=SIGMOID)
 
-        idle_values = keep.tile([P, P * PACK], BF16, align_bytes=64)
+        idle_words = keep.tile([P, P * PACK // 2], F32, align_bytes=64)
         idle_codes = keep.tile([P, P], U32, align_bytes=64)
         idle_scales = keep.tile([P, P], U8, align_bytes=64)
-        nc.vector.memset(idle_values[:], 0.0)
+        nc.vector.memset(idle_words[:], 0.0)
         nc.vector.quantize_mx(
-            out=idle_codes[:].bitcast(FP8X4), scales=idle_scales[:], in_=idle_values[:]
+            out=idle_codes[:].bitcast(FP8X4), scales=idle_scales[:], in_=idle_words[:].bitcast(BF16)
         )
         idle_bank = psum.tile([P, PACK, P], F32, tag="bank")
 

@@ -17,8 +17,8 @@ FEATURES = 512
 OUT_FEATURES = 128
 GROUPS = NODES // P
 PAIR = 2
-IDLE_WHILE_LOADING = 18
-IDLE_AFTER_TRANSPOSES = 4
+IDLE_WHILE_LOADING = 17
+IDLE_AFTER_TRANSPOSES = 3
 
 FLOPS = 2 * NODES * NODES * FEATURES + 2 * NODES * FEATURES * OUT_FEATURES
 
@@ -46,16 +46,16 @@ def tile_gcn_kron_pb_s_kernel(tc, h4, A, W4, t5_out, a5_out, z_out):
         w4_rows = keep.tile([P, PACK, OUT_FEATURES], BF16)
         nc.sync.dma_start(out=w4_rows[:], in_=W4.rearrange("(t p) d -> p t d", p=P))
 
+        idle_words = keep.tile([P, P * PACK // 2], F32, align_bytes=64)
+        nc.gpsimd.memset(idle_words[:], 0.0)
         table_warmer = keep.tile([P, 1], F32)
-        nc.gpsimd.memset(table_warmer[:], 0.0)
+        nc.vector.memset(table_warmer[:], 0.0)
         nc.scalar.activation(out=table_warmer[:], in_=table_warmer[:], func=SIGMOID)
         ident = keep.tile([P, P], F32)
         make_identity(nc, ident[:])
 
-        idle_words = keep.tile([P, P * PACK // 2], F32, align_bytes=64)
         idle_codes = keep.tile([P, P], U32, align_bytes=64)
         idle_scales = keep.tile([P, P], U8, align_bytes=64)
-        nc.vector.memset(idle_words[:], 0.0)
         nc.vector.quantize_mx(
             out=idle_codes[:].bitcast(FP8X4), scales=idle_scales[:], in_=idle_words[:].bitcast(BF16)
         )

@@ -40,9 +40,9 @@ def tile_gcn_kron_pb_s_kernel(tc, h4, A, W4, t5_out, a5_out, z_out):
             in_=h4.rearrange("(u p e) c -> p u e c", p=P, e=2),
         )
         a_rows = keep.tile([P, GROUPS, NODES], BF16)
-        a_view = A.rearrange("(r j) k -> r j k", j=GROUPS)
+        a_view = A.rearrange("(b r e) k -> r b e k", r=P, e=PAIR)
         for j in range(GROUPS):
-            nc.sync.dma_start(out=a_rows[:, j, :], in_=a_view[:, j, :])
+            nc.sync.dma_start(out=a_rows[:, j, :], in_=a_view[:, j // PAIR, j % PAIR, :])
         w4_rows = keep.tile([P, PACK, OUT_FEATURES], BF16)
         nc.sync.dma_start(out=w4_rows[:], in_=W4.rearrange("(t p) d -> p t d", p=P))
 
@@ -128,7 +128,7 @@ def tile_gcn_kron_pb_s_kernel(tc, h4, A, W4, t5_out, a5_out, z_out):
         )
 
         t5_sb = keep.tile([P, GROUPS, FEATURES], F32)
-        t5_view = t5_out.rearrange("(r j) f -> r j f", j=GROUPS)
+        t5_view = t5_out.rearrange("(b r e) f -> r b e f", r=P, e=PAIR)
         t5t_grouped = keep.tile([P, GROUPS, P, PACK], BF16, align_bytes=64)
         t5t_codes = keep.tile([P, NODES], U32, align_bytes=64)
         t5t_scales = keep.tile([P, NODES], U8, align_bytes=64)
@@ -166,7 +166,7 @@ def tile_gcn_kron_pb_s_kernel(tc, h4, A, W4, t5_out, a5_out, z_out):
                 stop=True,
             )
             nc.scalar.copy(out=t5_sb[:, j, :], in_=t5_bank[:])
-            nc.sync.dma_start(out=t5_view[:, j, :], in_=t5_sb[:, j, :])
+            nc.sync.dma_start(out=t5_view[:, j // PAIR, j % PAIR, :], in_=t5_sb[:, j, :])
             if j > 0:
                 quantise_t5t(j - 1)
             else:
@@ -179,8 +179,8 @@ def tile_gcn_kron_pb_s_kernel(tc, h4, A, W4, t5_out, a5_out, z_out):
 
         a5_sb = keep.tile([P, GROUPS, OUT_FEATURES], F32)
         z_sb = keep.tile([P, GROUPS, OUT_FEATURES], F32)
-        a5_view = a5_out.rearrange("(r j) d -> r j d", j=GROUPS)
-        z_view = z_out.rearrange("(r j) d -> r j d", j=GROUPS)
+        a5_view = a5_out.rearrange("(b r e) d -> r b e d", r=P, e=PAIR)
+        z_view = z_out.rearrange("(b r e) d -> r b e d", r=P, e=PAIR)
         for b in range(GROUPS // PAIR):
             a5_for_z = psum.tile([P, PAIR, OUT_FEATURES], F32, tag="bank")
             a5_for_store = psum.tile([P, PAIR, OUT_FEATURES], F32, tag="bank")
@@ -198,6 +198,6 @@ def tile_gcn_kron_pb_s_kernel(tc, h4, A, W4, t5_out, a5_out, z_out):
                     )
             groups = block(b, PAIR)
             nc.scalar.activation(out=z_sb[:, groups, :], in_=a5_for_z[:], func=SIGMOID)
-            nc.sync.dma_start(out=z_view[:, groups, :], in_=z_sb[:, groups, :])
+            nc.sync.dma_start(out=z_view[:, b, :, :], in_=z_sb[:, groups, :])
             nc.vector.tensor_copy(out=a5_sb[:, groups, :], in_=a5_for_store[:])
-            nc.sync.dma_start(out=a5_view[:, groups, :], in_=a5_sb[:, groups, :])
+            nc.sync.dma_start(out=a5_view[:, b, :, :], in_=a5_sb[:, groups, :])

from contextlib import ExitStack

import concourse.mybir as mybir
from concourse.masks import make_identity

BF16 = mybir.dt.bfloat16
F32 = mybir.dt.float32
U32 = mybir.dt.uint32
U8 = mybir.dt.uint8
FP8X4 = mybir.dt.float8_e4m3fn_x4
SIGMOID = mybir.ActivationFunctionType.Sigmoid

P = 128
PACK = 4
NODES = 512
FEATURES = 512
OUT_FEATURES = 128
GROUPS = NODES // P
PAIR = 2
IDLE_WHILE_LOADING = 17
IDLE_AFTER_TRANSPOSES = 3

FLOPS = 2 * NODES * NODES * FEATURES + 2 * NODES * FEATURES * OUT_FEATURES


def block(i, width=P):
    return slice(i * width, (i + 1) * width)


def tile_gcn_kron_pb_s_kernel(tc, h4, A, W4, t5_out, a5_out, z_out):
    nc = tc.nc
    with ExitStack() as ctx:
        keep = ctx.enter_context(tc.tile_pool(name="keep", bufs=1))
        psum = ctx.enter_context(tc.psum_pool(name="psum", bufs=8))
        ctx.enter_context(tc.manual_schedule())

        h4_rows = keep.tile([P, PACK, FEATURES], BF16)
        nc.sync.dma_start(
            out=h4_rows[:].rearrange("p (u e) c -> p u e c", e=2),
            in_=h4.rearrange("(u p e) c -> p u e c", p=P, e=2),
        )
        a_rows = keep.tile([P, GROUPS, NODES], BF16)
        a_view = A.rearrange("(b r e) k -> r b e k", r=P, e=PAIR)
        for j in range(GROUPS):
            nc.sync.dma_start(out=a_rows[:, j, :], in_=a_view[:, j // PAIR, j % PAIR, :])
        w4_rows = keep.tile([P, PACK, OUT_FEATURES], BF16)
        nc.sync.dma_start(out=w4_rows[:], in_=W4.rearrange("(t p) d -> p t d", p=P))

        idle_words = keep.tile([P, P * PACK // 2], F32, align_bytes=64)
        nc.gpsimd.memset(idle_words[:], 0.0)
        table_warmer = keep.tile([P, 1], F32)
        nc.vector.memset(table_warmer[:], 0.0)
        nc.scalar.activation(out=table_warmer[:], in_=table_warmer[:], func=SIGMOID)
        ident = keep.tile([P, P], F32)
        make_identity(nc, ident[:])

        idle_codes = keep.tile([P, P], U32, align_bytes=64)
        idle_scales = keep.tile([P, P], U8, align_bytes=64)
        nc.vector.quantize_mx(
            out=idle_codes[:].bitcast(FP8X4), scales=idle_scales[:], in_=idle_words[:].bitcast(BF16)
        )
        idle_bank = psum.tile([P, PACK, P], F32, tag="bank")

        def idle_passes(count):
            for i in range(count):
                nc.tensor.matmul_mx(
                    out=idle_bank[:, i % PACK, :],
                    lhsT=idle_codes[:].bitcast(FP8X4),
                    lhsT_scale=idle_scales[:],
                    rhs=idle_codes[:].bitcast(FP8X4),
                    rhs_scale=idle_scales[:],
                    start=True,
                    stop=True,
                )

        idle_passes(IDLE_WHILE_LOADING)

        h4_grouped = keep.tile([P, FEATURES, PACK], BF16, align_bytes=64)
        h4_codes = keep.tile([P, FEATURES], U32, align_bytes=64)
        h4_scales = keep.tile([P, FEATURES], U8, align_bytes=64)
        eighth = FEATURES // 8
        for copy, cols in (
            (nc.vector.tensor_copy, slice(0, 4 * eighth)),
            (nc.vector.tensor_copy, slice(4 * eighth, 5 * eighth)),
            (nc.scalar.copy, slice(5 * eighth, FEATURES)),
        ):
            copy(
                out=h4_grouped[:, cols, :].rearrange("p (c i) t -> p c t i", i=4),
                in_=h4_rows[:, :, cols].rearrange("p t (c i) -> p c t i", i=4),
            )
        for cols in (slice(0, 4 * eighth), slice(4 * eighth, FEATURES)):
            nc.vector.quantize_mx(
                out=h4_codes[:, cols].bitcast(FP8X4),
                scales=h4_scales[:, cols],
                in_=h4_grouped[:, cols, :].rearrange("p c t -> p (c t)"),
            )

        a_words = a_rows[:].rearrange("r j k -> r (j k)").bitcast(F32)
        words_per_row = NODES // 2
        at_grouped = keep.tile([P, GROUPS * P * PACK], BF16, align_bytes=64)
        at_grouped_words = at_grouped[:].bitcast(F32).rearrange(
            "p (j r u) -> p j r u", j=GROUPS, u=2
        )
        at_codes = keep.tile([P, NODES], U32, align_bytes=64)
        at_scales = keep.tile([P, NODES], U8, align_bytes=64)
        for j in range(GROUPS):
            at_bank = psum.tile([P, 2, P], F32, tag="bank")
            for u in range(2):
                first = j * words_per_row + u * P
                nc.tensor.transpose(at_bank[:, u, :], a_words[:, first : first + P], ident[:])
            nc.scalar.copy(
                out=at_grouped_words[:, j, :, :], in_=at_bank[:].rearrange("p u r -> p r u")
            )
        idle_passes(IDLE_AFTER_TRANSPOSES)
        for j in range(GROUPS):
            nc.vector.quantize_mx(
                out=at_codes[:, block(j)].bitcast(FP8X4),
                scales=at_scales[:, block(j)],
                in_=at_grouped[:, block(j, P * PACK)],
            )

        w4_grouped = keep.tile([P, OUT_FEATURES, PACK], BF16, align_bytes=64)
        w4_codes = keep.tile([P, OUT_FEATURES], U32, align_bytes=64)
        w4_scales = keep.tile([P, OUT_FEATURES], U8, align_bytes=64)
        nc.scalar.copy(
            out=w4_grouped[:].rearrange("p (d i) t -> p d t i", i=4),
            in_=w4_rows[:].rearrange("p t (d i) -> p d t i", i=4),
        )

        t5_sb = keep.tile([P, GROUPS, FEATURES], F32)
        t5_view = t5_out.rearrange("(b r e) f -> r b e f", r=P, e=PAIR)
        t5t_grouped = keep.tile([P, GROUPS, P, PACK], BF16, align_bytes=64)
        t5t_codes = keep.tile([P, NODES], U32, align_bytes=64)
        t5t_scales = keep.tile([P, NODES], U8, align_bytes=64)

        def quantise_t5t(j):
            nc.vector.quantize_mx(
                out=t5t_codes[:, block(j)].bitcast(FP8X4),
                scales=t5t_scales[:, block(j)],
                in_=t5t_grouped[:, j, :, :].rearrange("p r t -> p (r t)"),
            )

        for j in range(GROUPS):
            t5t_bank = psum.tile([P, PACK, P], F32, tag="bank")
            for t in range(PACK):
                nc.tensor.matmul_mx(
                    out=t5t_bank[:, t, :],
                    lhsT=h4_codes[:, block(t)].bitcast(FP8X4),
                    lhsT_scale=h4_scales[:, block(t)],
                    rhs=at_codes[:, block(j)].bitcast(FP8X4),
                    rhs_scale=at_scales[:, block(j)],
                    start=True,
                    stop=True,
                )
            nc.vector.tensor_copy(
                out=t5t_grouped[:, j, :, :], in_=t5t_bank[:].rearrange("p t r -> p r t")
            )
            t5_bank = psum.tile([P, FEATURES], F32, tag="bank")
            nc.tensor.matmul_mx(
                out=t5_bank[:],
                lhsT=at_codes[:, block(j)].bitcast(FP8X4),
                lhsT_scale=at_scales[:, block(j)],
                rhs=h4_codes[:].bitcast(FP8X4),
                rhs_scale=h4_scales[:],
                start=True,
                stop=True,
            )
            nc.scalar.copy(out=t5_sb[:, j, :], in_=t5_bank[:])
            nc.sync.dma_start(out=t5_view[:, j // PAIR, j % PAIR, :], in_=t5_sb[:, j, :])
            if j > 0:
                quantise_t5t(j - 1)
            else:
                nc.vector.quantize_mx(
                    out=w4_codes[:].bitcast(FP8X4),
                    scales=w4_scales[:],
                    in_=w4_grouped[:].rearrange("p d t -> p (d t)"),
                )
        quantise_t5t(GROUPS - 1)

        a5_sb = keep.tile([P, GROUPS, OUT_FEATURES], F32)
        z_sb = keep.tile([P, GROUPS, OUT_FEATURES], F32)
        a5_view = a5_out.rearrange("(b r e) d -> r b e d", r=P, e=PAIR)
        z_view = z_out.rearrange("(b r e) d -> r b e d", r=P, e=PAIR)
        for b in range(GROUPS // PAIR):
            a5_for_z = psum.tile([P, PAIR, OUT_FEATURES], F32, tag="bank")
            a5_for_store = psum.tile([P, PAIR, OUT_FEATURES], F32, tag="bank")
            for jj in range(PAIR):
                j = b * PAIR + jj
                for a5_bank in (a5_for_z, a5_for_store):
                    nc.tensor.matmul_mx(
                        out=a5_bank[:, jj, :],
                        lhsT=t5t_codes[:, block(j)].bitcast(FP8X4),
                        lhsT_scale=t5t_scales[:, block(j)],
                        rhs=w4_codes[:].bitcast(FP8X4),
                        rhs_scale=w4_scales[:],
                        start=True,
                        stop=True,
                    )
            groups = block(b, PAIR)
            nc.scalar.activation(out=z_sb[:, groups, :], in_=a5_for_z[:], func=SIGMOID)
            nc.sync.dma_start(out=z_view[:, b, :, :], in_=z_sb[:, groups, :])
            nc.vector.tensor_copy(out=a5_sb[:, groups, :], in_=a5_for_store[:])
            nc.sync.dma_start(out=a5_view[:, b, :, :], in_=a5_sb[:, groups, :])
